import numpy as np
import ml_dtypes


def mxq(x, axis, fmt="e4m3"):
    dtype, down = {"e4m3": (ml_dtypes.float8_e4m3fn, 7), "e5m2": (ml_dtypes.float8_e5m2, 14)}[fmt]
    v = np.moveaxis(np.asarray(x, np.float32).astype(ml_dtypes.bfloat16).astype(np.float64), axis, -1)
    blocks = v.reshape(v.shape[:-1] + (-1, 32))
    amax = np.abs(blocks).max(-1, keepdims=True)
    byte = np.maximum(np.where(amax > 0, np.frexp(amax)[1] - 1 + 127, 0) - down, 1)
    scale = np.exp2(byte - 127.0)
    codes = (blocks / scale).astype(np.float32).astype(dtype).astype(np.float64)
    return np.moveaxis((codes * scale).reshape(v.shape), -1, axis)


WIDE = False


def mx_kscale(k):
    if not WIDE:
        return np.ones(k)
    levels = np.array([10, -10, 5, -5, 0])
    if k % 512:
        return np.exp2(np.random.permutation(np.resize(levels, k // 32))).repeat(32)
    a = np.empty((k // 512, 16))
    for p in range(k // 512):
        a[p, :8] = np.random.permutation(np.resize(levels, 8))
        for g in range(8):
            far = levels[np.abs(levels - a[p, g]) >= 10]
            a[p, g + 8] = far[np.random.randint(len(far))]
    return np.exp2(a.ravel()).repeat(32)


BF16 = ml_dtypes.bfloat16


def bf(x):
    return np.asarray(x, np.float32).astype(BF16)


def f64(x):
    return np.asarray(x).astype(np.float64)


B, N, P, D, H = 2, 2048, 4, 512, 16
E = P * D
DH = E // H


def sincos_table(n, e):
    pe = np.zeros((n, e))
    position = np.arange(n, dtype=np.float64)[:, None]
    div_term = np.exp(np.arange(0, e, 2, dtype=np.float64) * -(np.log(10000.0) / e))
    pe[:, 0::2] = np.sin(position * div_term)
    pe[:, 1::2] = np.cos(position * div_term)
    pe = pe - pe.mean()
    return pe / (pe.std() * 10)


def setup_inputs():
    s, t = mx_kscale(E), mx_kscale(E)
    c = 1.0 / np.sqrt(E)
    return {"x": bf(np.random.standard_normal((B, N, P, D)) * s.reshape(P, D)),
            "pos_embed": bf(sincos_table(N, E) * t),
            "W_embed": bf(np.random.standard_normal((E, E)) * c * t[:, None] / s),
            "b_embed": bf(np.random.standard_normal(E) * 0.1 * t),
            "Wq": bf(np.random.standard_normal((E, E)) * c / t),
            "bq": bf(np.random.standard_normal(E) * 0.1),
            "Wk": bf(np.random.standard_normal((E, E)) * c / t),
            "bk": bf(np.random.standard_normal(E) * 0.1),
            "Wv": bf(np.random.standard_normal((E, E)) * c / t),
            "bv": bf(np.random.standard_normal(E) * 0.1)}


def reference(x, pos_embed, W_embed, b_embed, Wq, bq, Wk, bk, Wv, bv):
    xf = f64(x).reshape(B, N, E)
    xe = (mxq(xf, 2, "e4m3") @ mxq(f64(W_embed).T, 0, "e4m3")) + f64(b_embed)
    xe = xe + f64(pos_embed)
    xq = mxq(xe, 2, "e4m3")
    q = ((xq @ mxq(f64(Wq).T, 0, "e4m3")) + f64(bq)).reshape(B, N, H, DH)
    k = ((xq @ mxq(f64(Wk).T, 0, "e4m3")) + f64(bk)).reshape(B, N, H, DH)
    v = ((xq @ mxq(f64(Wv).T, 0, "e4m3")) + f64(bv)).reshape(B, N, H, DH)
    return q, k, v

@@ -1,0 +1,288 @@
+from contextlib import ExitStack
+
+import concourse.mybir as mybir
+from concourse.masks import make_identity
+
+F32 = mybir.dt.float32
+BF16 = mybir.dt.bfloat16
+U32 = mybir.dt.uint32
+U8 = mybir.dt.uint8
+FP8X4 = mybir.dt.float8_e4m3fn_x4
+ADD = mybir.AluOpType.add
+
+P = 128
+E = 2048
+NPOS = 2048
+NTB = 8
+FLOPS = 4 * 2 * 4096 * 2048 * 2048
+
+
+def tile_attention_pa_l_kernel(
+    tc, x, pos_embed, W_embed, b_embed, Wq, bq, Wk, bk, Wv, bv, out_0, out_1, out_2
+):
+    nc = tc.nc
+    xf = x.rearrange("b n p d -> (b n) (p d)")
+    outs = [o.rearrange("b n h d -> (b n) (h d)") for o in (out_0, out_1, out_2)]
+    w2 = [Wq, Wk, Wv]
+    b2 = [bq, bk, bv]
+
+    with ExitStack() as ctx:
+        const = ctx.enter_context(tc.tile_pool(name="const", bufs=1))
+        p_codes = ctx.enter_context(tc.tile_pool(name="codes", bufs=14))
+        p_raw = ctx.enter_context(tc.tile_pool(name="raw", bufs=4))
+        p_srt = ctx.enter_context(tc.tile_pool(name="srt", bufs=2))
+        p_grp = ctx.enter_context(tc.tile_pool(name="grp", bufs=2))
+        p_pos = ctx.enter_context(tc.tile_pool(name="pos", bufs=2))
+        p_st = ctx.enter_context(tc.tile_pool(name="st", bufs=5))
+        ps_t = ctx.enter_context(tc.psum_pool(name="pst", bufs=4))
+        ps_a = ctx.enter_context(tc.psum_pool(name="psa", bufs=4))
+
+        ident = const.tile([P, P], F32, name="ident")
+        make_identity(nc, ident[:])
+        be_raw = const.tile([P, 4, 4], BF16, name="be_raw")
+        be = const.tile([P, 16], F32, name="be")
+        bias = const.tile([P, 3 * E], BF16, name="bias")
+        warm = const.tile([P, 1], F32, name="warm")
+        warm2 = const.tile([P, 1], F32, name="warm2")
+
+        ctx.enter_context(tc.manual_schedule())
+
+        nc.vector.memset(warm[:], 0.0)
+        nc.scalar.copy(out=warm2[:], in_=warm[:])
+        nc.scalar.dma_start(out=be_raw[:], in_=b_embed.rearrange("(g p t) -> p g t", p=P, t=4))
+
+        runs = []
+
+        def add_run(kind, src, key, j):
+            runs.append({"kind": kind, "src": src, "key": key, "j": j})
+
+        def rows(ap, r0):
+            return ap[r0 : r0 + 256, :].rearrange("(tl p) k -> p tl k", p=P)
+
+        def add_x(tb):
+            for b in range(2):
+                add_run("q", rows(xf, b * NPOS + tb * 256), ("x", tb), b)
+
+        def add_we(gg):
+            view = W_embed[512 * gg : 512 * gg + 512, :].rearrange("(m t) k -> m t k", t=4)
+            for j in range(2):
+                add_run("q", view[:, 2 * j : 2 * j + 2, :], ("we", gg), j)
+
+        add_x(0)
+        add_we(0)
+        add_run("pos", rows(pos_embed, 0), ("pos", 0), 0)
+        for gg in range(1, 4):
+            add_we(gg)
+        for tb in range(1, NTB):
+            add_x(tb)
+            add_run("pos", rows(pos_embed, tb * 256), ("pos", tb), 0)
+        for wb in range(12):
+            for j in range(2):
+                add_run("q", rows(w2[wb // 4], (wb % 4) * 512 + 256 * j), ("w", wb), j)
+
+        blocks = {}
+        pend_v = []
+        pend_s = []
+
+        def new_block(key):
+            codes = p_codes.tile([P, 4, 512], U32, tag="codes", name="codes", align_bytes=64)
+            planes = p_codes.tile([P, 512], U8, tag="planes", name="planes", align_bytes=64)
+            blocks[key] = (codes, planes)
+            return blocks[key]
+
+        def pop_v():
+            item = pend_v.pop(0)
+            item[2]()
+
+        def need_block(key):
+            while any([it[0] == key for it in pend_v]):
+                pop_v()
+
+        def need_run(idx):
+            while any([it[1] == idx for it in pend_v]):
+                pop_v()
+
+        def flush_s():
+            while len(pend_s) > 0:
+                fn = pend_s.pop(0)
+                fn()
+
+        def emit_load(i):
+            if i >= len(runs):
+                return
+            raw = p_raw.tile([P, 2, E], BF16, tag="raw", name="raw")
+            nc.sync.dma_start(out=raw[:], in_=runs[i]["src"])
+            runs[i]["raw"] = raw
+
+        def emit_sort(i):
+            if i >= len(runs):
+                return
+            srt = p_srt.tile([P, 8, 2, P], F32, tag="srt", name="srt")
+            words = runs[i]["raw"][:].rearrange("p tl k -> p (tl k)").bitcast(F32)
+            nc.vector.tensor_copy(
+                out=srt[:], in_=words.rearrange("p (a w u) -> p a u w", a=8, u=2)
+            )
+            runs[i]["srt"] = srt
+
+        def quant(codes, planes, g, c0, width, src):
+            nc.vector.quantize_mx(
+                out=codes[:, g, c0 : c0 + width].bitcast(FP8X4),
+                scales=planes[4 * g : P, c0 : c0 + width],
+                in_=src,
+            )
+
+        def emit_run(i):
+            r = runs[i]
+            emit_load(i + 3)
+            emit_sort(i + 1)
+            need_run(i - 2)
+            srt = r["srt"]
+            if r["kind"] == "pos":
+                dst = p_pos.tile([P, 4, 1024], BF16, tag="pos", name="post")
+                blocks[r["key"]] = dst
+            else:
+                dst = p_grp.tile([P, 4, 1024], BF16, tag="grp", name="grp", align_bytes=64)
+            for g in range(4):
+                tp = ps_t.tile([P, 2, 256], F32, tag="tp", name="tp")
+                for u in range(2):
+                    for tl in range(2):
+                        nc.tensor.transpose(
+                            tp[:, u, tl * P : (tl + 1) * P], srt[:, tl * 4 + g, u, :], ident[:]
+                        )
+                nc.scalar.copy(
+                    out=dst[:, g, :].bitcast(F32).rearrange("p (r u) -> p r u", u=2),
+                    in_=tp[:].rearrange("p u r -> p r u"),
+                )
+            if r["kind"] == "q":
+                if r["j"] == 0:
+                    new_block(r["key"])
+                codes, planes = blocks[r["key"]]
+                for g in range(4):
+                    pend_v.append(
+                        (
+                            r["key"],
+                            i,
+                            lambda g=g, codes=codes, planes=planes, dst=dst, c0=256 * r["j"]: quant(
+                                codes, planes, g, c0, 256, dst[:, g, :]
+                            ),
+                        )
+                    )
+            flush_s()
+
+        def after_unit():
+            for rep in range(2):
+                if len(pend_v) > 0:
+                    pop_v()
+
+        def mm4(acc, lc, lp, l0, rc, rp):
+            for g in range(4):
+                nc.tensor.matmul_mx(
+                    out=acc[:],
+                    lhsT=lc[:, g, l0 : l0 + P].bitcast(FP8X4),
+                    lhsT_scale=lp[4 * g : P, l0 : l0 + P],
+                    rhs=rc[:, g, :].bitcast(FP8X4),
+                    rhs_scale=rp[4 * g : P, :],
+                    start=(g == 0),
+                    stop=(g == 3),
+                )
+
+        cur = {}
+
+        def interleave(tb, gg, xeb):
+            xg = p_st.tile([P, 2048], BF16, tag="st", name="xg", align_bytes=64)
+            nc.scalar.copy(
+                out=xg[:].rearrange("p (n t) -> p n t", t=4),
+                in_=xeb[:].rearrange("p t n -> p n t"),
+            )
+            if gg == 0:
+                new_block(("xe", tb))
+            codes, planes = blocks[("xe", tb)]
+            pend_v.append((("xe", tb), -1, lambda: quant(codes, planes, gg, 0, 512, xg[:])))
+
+        def emit_s1(tb, gg, t):
+            if t == 0:
+                flush_s()
+                need_block(("x", tb))
+                need_block(("we", gg))
+                cur["xeb"] = p_st.tile([P, 4, 512], BF16, tag="st", name="xeb", align_bytes=64)
+            xeb = cur["xeb"]
+            wc, wp = blocks[("we", gg)]
+            xc, xp = blocks[("x", tb)]
+            acc = ps_a.tile([P, 512], F32, tag="acc", name="acc")
+            mm4(acc, wc, wp, P * t, xc, xp)
+            post = blocks[("pos", tb)]
+            pos_t = post[:, gg, :].rearrange("p (r t) -> p r t", t=4)[:, :, t]
+            nc.vector.scalar_tensor_tensor(
+                out=xeb[:, t, :].rearrange("p (b r) -> p b r", b=2),
+                in0=acc[:].rearrange("p (b r) -> p b r", b=2),
+                scalar=be[:, 4 * gg + t : 4 * gg + t + 1],
+                in1=pos_t.unsqueeze(1).to_broadcast([P, 2, 256]),
+                op0=ADD,
+                op1=ADD,
+            )
+            after_unit()
+            if t == 3:
+                pend_s.append(lambda: interleave(tb, gg, xeb))
+
+        def emit_s2(wb, tt):
+            tb = tt // 4
+            q = tt % 4
+            if tt == 0:
+                need_block(("w", wb))
+            if q == 0:
+                flush_s()
+                need_block(("xe", tb))
+            if q % 2 == 0:
+                cur["ost"] = p_st.tile([P, 2, 512], F32, tag="st", name="ost", align_bytes=64)
+            ost = cur["ost"]
+            xc, xp = blocks[("xe", tb)]
+            wc, wp = blocks[("w", wb)]
+            acc = ps_a.tile([P, 512], F32, tag="acc", name="acc")
+            mm4(acc, xc, xp, P * q, wc, wp)
+            nc.vector.tensor_tensor(
+                out=ost[:, q % 2, :], in0=acc[:], in1=bias[:, 512 * wb : 512 * wb + 512], op=ADD
+            )
+            after_unit()
+            if q % 2 == 1:
+                r0 = (q // 2) * NPOS + tb * 256
+                c0 = (wb % 4) * 512
+                nc.sync.dma_start(
+                    out=outs[wb // 4][r0 : r0 + 256, c0 : c0 + 512].rearrange(
+                        "(h p) c -> p h c", p=P
+                    ),
+                    in_=ost[:],
+                )
+
+        for i in range(3):
+            emit_load(i)
+        nc.vector.tensor_copy(out=be[:], in_=be_raw[:].rearrange("p g t -> p (g t)"))
+        emit_sort(0)
+        nxt = [0]
+
+        def run_next():
+            emit_run(nxt[0])
+            nxt[0] = nxt[0] + 1
+
+        for i in range(7):
+            run_next()
+        for gg in range(4):
+            for t in range(4):
+                emit_s1(0, gg, t)
+                if t == 1 or (t == 3 and gg < 3):
+                    run_next()
+        for tb in range(1, NTB):
+            for gg in range(4):
+                if gg < 3 and not (tb == NTB - 1 and gg == 2):
+                    run_next()
+                if tb == 2 and gg == 3:
+                    for wi in range(3):
+                        nc.sync.dma_start(
+                            out=bias[:, wi * E : (wi + 1) * E], in_=b2[wi].partition_broadcast(P)
+                        )
+                for t in range(4):
+                    emit_s1(tb, gg, t)
+        for wb in range(12):
+            for tt in range(32):
+                if wb < 11 and tt % 16 == 0:
+                    run_next()
+                emit_s2(wb, tt)

@@ -239,9 +239,12 @@ def tile_attention_pa_l_kernel(
             wc, wp = blocks[("w", wb)]
             acc = ps_a.tile([P, 512], F32, tag="acc", name="acc")
             mm4(acc, xc, xp, P * q, wc, wp)
-            nc.vector.tensor_tensor(
-                out=ost[:, q % 2, :], in0=acc[:], in1=bias[:, 512 * wb : 512 * wb + 512], op=ADD
-            )
+            b_ap = bias[:, 512 * wb : 512 * wb + 512]
+            if q % 2 == 0:
+                nc.vector.tensor_tensor(out=ost[:, 0, :], in0=acc[:], in1=b_ap, op=ADD)
+            else:
+                nc.scalar.copy(out=ost[:, 1, :], in_=acc[:])
+                nc.vector.tensor_tensor(out=ost[:, 1, :], in0=ost[:, 1, :], in1=b_ap, op=ADD)
             after_unit()
             if q % 2 == 1:
                 r0 = (q // 2) * NPOS + tb * 256
@@ -255,7 +258,6 @@ def tile_attention_pa_l_kernel(
 
         for i in range(3):
             emit_load(i)
-        nc.vector.tensor_copy(out=be[:], in_=be_raw[:].rearrange("p g t -> p (g t)"))
         emit_sort(0)
         nxt = [0]
 
@@ -265,6 +267,7 @@ def tile_attention_pa_l_kernel(
 
         for i in range(7):
             run_next()
+        nc.vector.tensor_copy(out=be[:], in_=be_raw[:].rearrange("p g t -> p (g t)"))
         for gg in range(4):
             for t in range(4):
                 emit_s1(0, gg, t)

@@ -115,8 +115,6 @@ def tile_attention_pa_l_kernel(
             runs[i]["raw"] = raw
 
         def emit_sort(i):
-            if i >= len(runs):
-                return
             srt = p_srt.tile([P, 8, 2, P], F32, tag="srt", name="srt")
             words = runs[i]["raw"][:].rearrange("p tl k -> p (tl k)").bitcast(F32)
             nc.vector.tensor_copy(
@@ -131,42 +129,55 @@ def tile_attention_pa_l_kernel(
                 in_=src,
             )
 
-        def emit_run(i):
-            r = runs[i]
-            emit_load(i + 3)
-            emit_sort(i + 1)
-            need_run(i - 2)
-            srt = r["srt"]
-            if r["kind"] == "pos":
-                dst = p_pos.tile([P, 4, 1024], BF16, tag="pos", name="post")
-                blocks[r["key"]] = dst
-            else:
-                dst = p_grp.tile([P, 4, 1024], BF16, tag="grp", name="grp", align_bytes=64)
-            for g in range(4):
-                tp = ps_t.tile([P, 2, 256], F32, tag="tp", name="tp")
-                for u in range(2):
-                    for tl in range(2):
-                        nc.tensor.transpose(
-                            tp[:, u, tl * P : (tl + 1) * P], srt[:, tl * 4 + g, u, :], ident[:]
-                        )
-                nc.scalar.copy(
-                    out=dst[:, g, :].bitcast(F32).rearrange("p (r u) -> p r u", u=2),
-                    in_=tp[:].rearrange("p u r -> p r u"),
-                )
-            if r["kind"] == "q":
-                if r["j"] == 0:
-                    new_block(r["key"])
-                codes, planes = blocks[r["key"]]
+        def emit_sr(k):
+            idxs = srs[k]
+            for i in idxs:
+                need_block(("sort", i))
+                need_run(i - 2)
+            for i in idxs:
+                emit_load(i + 4)
+            dsts = []
+            for n, i in enumerate(idxs):
+                r = runs[i]
+                srt = r["srt"]
+                if r["kind"] == "pos":
+                    dst = p_pos.tile([P, 4, 1024], BF16, tag="pos", name="post")
+                    blocks[r["key"]] = dst
+                else:
+                    dst = p_grp.tile([P, 4, 1024], BF16, tag="grp", name="grp", align_bytes=64)
+                dsts.append(dst)
                 for g in range(4):
-                    pend_v.append(
-                        (
-                            r["key"],
-                            i,
-                            lambda g=g, codes=codes, planes=planes, dst=dst, c0=256 * r["j"]: quant(
-                                codes, planes, g, c0, 256, dst[:, g, :]
-                            ),
+                    tp = ps_t.tile([P, 2, 256], F32, tag="tp", name="tp")
+                    for u in range(2):
+                        for tl in range(2):
+                            nc.tensor.transpose(
+                                tp[:, u, tl * P : (tl + 1) * P], srt[:, tl * 4 + g, u, :], ident[:]
+                            )
+                    o_ap = dst[:, g, :].bitcast(F32).rearrange("p (r u) -> p r u", u=2)
+                    i_ap = tp[:].rearrange("p u r -> p r u")
+                    if len(idxs) == 2 and n == 0 and g == 1:
+                        nc.vector.tensor_copy(out=o_ap, in_=i_ap)
+                    else:
+                        nc.scalar.copy(out=o_ap, in_=i_ap)
+            following = srs[k + 1] if k + 1 < len(srs) else []
+            for n in range(max(len(idxs), len(following))):
+                if n < len(following):
+                    pend_v.append((("sort", following[n]), -1, lambda i=following[n]: emit_sort(i)))
+                if n < len(idxs) and runs[idxs[n]]["kind"] == "q":
+                    r = runs[idxs[n]]
+                    if r["j"] == 0:
+                        new_block(r["key"])
+                    codes, planes = blocks[r["key"]]
+                    for g in range(4):
+                        pend_v.append(
+                            (
+                                r["key"],
+                                idxs[n],
+                                lambda g=g, codes=codes, planes=planes, dst=dsts[n], c0=256 * r["j"]: quant(
+                                    codes, planes, g, c0, 256, dst[:, g, :]
+                                ),
+                            )
                         )
-                    )
             flush_s()
 
         def after_unit():
@@ -239,12 +250,9 @@ def tile_attention_pa_l_kernel(
             wc, wp = blocks[("w", wb)]
             acc = ps_a.tile([P, 512], F32, tag="acc", name="acc")
             mm4(acc, xc, xp, P * q, wc, wp)
-            b_ap = bias[:, 512 * wb : 512 * wb + 512]
-            if q % 2 == 0:
-                nc.vector.tensor_tensor(out=ost[:, 0, :], in0=acc[:], in1=b_ap, op=ADD)
-            else:
-                nc.scalar.copy(out=ost[:, 1, :], in_=acc[:])
-                nc.vector.tensor_tensor(out=ost[:, 1, :], in0=ost[:, 1, :], in1=b_ap, op=ADD)
+            nc.vector.tensor_tensor(
+                out=ost[:, q % 2, :], in0=acc[:], in1=bias[:, 512 * wb : 512 * wb + 512], op=ADD
+            )
             after_unit()
             if q % 2 == 1:
                 r0 = (q // 2) * NPOS + tb * 256
@@ -256,27 +264,39 @@ def tile_attention_pa_l_kernel(
                     in_=ost[:],
                 )
 
-        for i in range(3):
+        srs = []
+        i = 0
+        while i < len(runs):
+            if runs[i]["kind"] == "pos":
+                srs.append([i])
+                i = i + 1
+            else:
+                srs.append([i, i + 1])
+                i = i + 2
+        for i in range(4):
             emit_load(i)
         emit_sort(0)
+        emit_sort(1)
         nxt = [0]
 
-        def run_next():
-            emit_run(nxt[0])
+        def sr_next():
+            emit_sr(nxt[0])
             nxt[0] = nxt[0] + 1
 
-        for i in range(7):
-            run_next()
+        for i in range(4):
+            sr_next()
         nc.vector.tensor_copy(out=be[:], in_=be_raw[:].rearrange("p g t -> p (g t)"))
         for gg in range(4):
             for t in range(4):
+                if gg == 3 and t == 2:
+                    sr_next()
                 emit_s1(0, gg, t)
-                if t == 1 or (t == 3 and gg < 3):
-                    run_next()
+            if gg < 3:
+                sr_next()
         for tb in range(1, NTB):
             for gg in range(4):
-                if gg < 3 and not (tb == NTB - 1 and gg == 2):
-                    run_next()
+                if gg == 0 or (gg == 2 and tb < NTB - 1):
+                    sr_next()
                 if tb == 2 and gg == 3:
                     for wi in range(3):
                         nc.sync.dma_start(
@@ -286,6 +306,6 @@ def tile_attention_pa_l_kernel(
                     emit_s1(tb, gg, t)
         for wb in range(12):
             for tt in range(32):
-                if wb < 11 and tt % 16 == 0:
-                    run_next()
+                if wb < 11 and tt == 0:
+                    sr_next()
                 emit_s2(wb, tt)

from contextlib import ExitStack

import concourse.mybir as mybir
from concourse.masks import make_identity

F32 = mybir.dt.float32
BF16 = mybir.dt.bfloat16
U32 = mybir.dt.uint32
U8 = mybir.dt.uint8
FP8X4 = mybir.dt.float8_e4m3fn_x4
ADD = mybir.AluOpType.add

P = 128
E = 2048
NPOS = 2048
NTB = 8
FLOPS = 4 * 2 * 4096 * 2048 * 2048


def tile_attention_pa_l_kernel(
    tc, x, pos_embed, W_embed, b_embed, Wq, bq, Wk, bk, Wv, bv, out_0, out_1, out_2
):
    nc = tc.nc
    xf = x.rearrange("b n p d -> (b n) (p d)")
    outs = [o.rearrange("b n h d -> (b n) (h d)") for o in (out_0, out_1, out_2)]
    w2 = [Wq, Wk, Wv]
    b2 = [bq, bk, bv]

    with ExitStack() as ctx:
        const = ctx.enter_context(tc.tile_pool(name="const", bufs=1))
        p_codes = ctx.enter_context(tc.tile_pool(name="codes", bufs=14))
        p_raw = ctx.enter_context(tc.tile_pool(name="raw", bufs=4))
        p_srt = ctx.enter_context(tc.tile_pool(name="srt", bufs=2))
        p_grp = ctx.enter_context(tc.tile_pool(name="grp", bufs=2))
        p_pos = ctx.enter_context(tc.tile_pool(name="pos", bufs=2))
        p_st = ctx.enter_context(tc.tile_pool(name="st", bufs=5))
        ps_t = ctx.enter_context(tc.psum_pool(name="pst", bufs=4))
        ps_a = ctx.enter_context(tc.psum_pool(name="psa", bufs=4))

        ident = const.tile([P, P], F32, name="ident")
        make_identity(nc, ident[:])
        be_raw = const.tile([P, 4, 4], BF16, name="be_raw")
        be = const.tile([P, 16], F32, name="be")
        bias = const.tile([P, 3 * E], BF16, name="bias")
        warm = const.tile([P, 1], F32, name="warm")
        warm2 = const.tile([P, 1], F32, name="warm2")

        ctx.enter_context(tc.manual_schedule())

        nc.vector.memset(warm[:], 0.0)
        nc.scalar.copy(out=warm2[:], in_=warm[:])
        nc.scalar.dma_start(out=be_raw[:], in_=b_embed.rearrange("(g p t) -> p g t", p=P, t=4))

        runs = []

        def add_run(kind, src, key, j):
            runs.append({"kind": kind, "src": src, "key": key, "j": j})

        def rows(ap, r0):
            return ap[r0 : r0 + 256, :].rearrange("(tl p) k -> p tl k", p=P)

        def add_x(tb):
            for b in range(2):
                add_run("q", rows(xf, b * NPOS + tb * 256), ("x", tb), b)

        def add_we(gg):
            view = W_embed[512 * gg : 512 * gg + 512, :].rearrange("(m t) k -> m t k", t=4)
            for j in range(2):
                add_run("q", view[:, 2 * j : 2 * j + 2, :], ("we", gg), j)

        add_x(0)
        add_we(0)
        add_run("pos", rows(pos_embed, 0), ("pos", 0), 0)
        for gg in range(1, 4):
            add_we(gg)
        for tb in range(1, NTB):
            add_x(tb)
            add_run("pos", rows(pos_embed, tb * 256), ("pos", tb), 0)
        for wb in range(12):
            for j in range(2):
                add_run("q", rows(w2[wb // 4], (wb % 4) * 512 + 256 * j), ("w", wb), j)

        blocks = {}
        pend_v = []
        pend_s = []

        def new_block(key):
            codes = p_codes.tile([P, 4, 512], U32, tag="codes", name="codes", align_bytes=64)
            planes = p_codes.tile([P, 512], U8, tag="planes", name="planes", align_bytes=64)
            blocks[key] = (codes, planes)
            return blocks[key]

        def pop_v():
            item = pend_v.pop(0)
            item[2]()

        def need_block(key):
            while any([it[0] == key for it in pend_v]):
                pop_v()

        def need_run(idx):
            while any([it[1] == idx for it in pend_v]):
                pop_v()

        def flush_s():
            while len(pend_s) > 0:
                fn = pend_s.pop(0)
                fn()

        def emit_load(i):
            if i >= len(runs):
                return
            raw = p_raw.tile([P, 2, E], BF16, tag="raw", name="raw")
            nc.sync.dma_start(out=raw[:], in_=runs[i]["src"])
            runs[i]["raw"] = raw

        def emit_sort(i):
            srt = p_srt.tile([P, 8, 2, P], F32, tag="srt", name="srt")
            words = runs[i]["raw"][:].rearrange("p tl k -> p (tl k)").bitcast(F32)
            nc.vector.tensor_copy(
                out=srt[:], in_=words.rearrange("p (a w u) -> p a u w", a=8, u=2)
            )
            runs[i]["srt"] = srt

        def quant(codes, planes, g, c0, width, src):
            nc.vector.quantize_mx(
                out=codes[:, g, c0 : c0 + width].bitcast(FP8X4),
                scales=planes[4 * g : P, c0 : c0 + width],
                in_=src,
            )

        def emit_sr(k):
            idxs = srs[k]
            for i in idxs:
                need_block(("sort", i))
                need_run(i - 2)
            for i in idxs:
                emit_load(i + 4)
            dsts = []
            for n, i in enumerate(idxs):
                r = runs[i]
                srt = r["srt"]
                if r["kind"] == "pos":
                    dst = p_pos.tile([P, 4, 1024], BF16, tag="pos", name="post")
                    blocks[r["key"]] = dst
                else:
                    dst = p_grp.tile([P, 4, 1024], BF16, tag="grp", name="grp", align_bytes=64)
                dsts.append(dst)
                for g in range(4):
                    tp = ps_t.tile([P, 2, 256], F32, tag="tp", name="tp")
                    for u in range(2):
                        for tl in range(2):
                            nc.tensor.transpose(
                                tp[:, u, tl * P : (tl + 1) * P], srt[:, tl * 4 + g, u, :], ident[:]
                            )
                    o_ap = dst[:, g, :].bitcast(F32).rearrange("p (r u) -> p r u", u=2)
                    i_ap = tp[:].rearrange("p u r -> p r u")
                    if len(idxs) == 2 and n == 0 and g == 1:
                        nc.vector.tensor_copy(out=o_ap, in_=i_ap)
                    else:
                        nc.scalar.copy(out=o_ap, in_=i_ap)
            following = srs[k + 1] if k + 1 < len(srs) else []
            for n in range(max(len(idxs), len(following))):
                if n < len(following):
                    pend_v.append((("sort", following[n]), -1, lambda i=following[n]: emit_sort(i)))
                if n < len(idxs) and runs[idxs[n]]["kind"] == "q":
                    r = runs[idxs[n]]
                    if r["j"] == 0:
                        new_block(r["key"])
                    codes, planes = blocks[r["key"]]
                    for g in range(4):
                        pend_v.append(
                            (
                                r["key"],
                                idxs[n],
                                lambda g=g, codes=codes, planes=planes, dst=dsts[n], c0=256 * r["j"]: quant(
                                    codes, planes, g, c0, 256, dst[:, g, :]
                                ),
                            )
                        )
            flush_s()

        def after_unit():
            for rep in range(2):
                if len(pend_v) > 0:
                    pop_v()

        def mm4(acc, lc, lp, l0, rc, rp):
            for g in range(4):
                nc.tensor.matmul_mx(
                    out=acc[:],
                    lhsT=lc[:, g, l0 : l0 + P].bitcast(FP8X4),
                    lhsT_scale=lp[4 * g : P, l0 : l0 + P],
                    rhs=rc[:, g, :].bitcast(FP8X4),
                    rhs_scale=rp[4 * g : P, :],
                    start=(g == 0),
                    stop=(g == 3),
                )

        cur = {}

        def interleave(tb, gg, xeb):
            xg = p_st.tile([P, 2048], BF16, tag="st", name="xg", align_bytes=64)
            nc.scalar.copy(
                out=xg[:].rearrange("p (n t) -> p n t", t=4),
                in_=xeb[:].rearrange("p t n -> p n t"),
            )
            if gg == 0:
                new_block(("xe", tb))
            codes, planes = blocks[("xe", tb)]
            pend_v.append((("xe", tb), -1, lambda: quant(codes, planes, gg, 0, 512, xg[:])))

        def emit_s1(tb, gg, t):
            if t == 0:
                flush_s()
                need_block(("x", tb))
                need_block(("we", gg))
                cur["xeb"] = p_st.tile([P, 4, 512], BF16, tag="st", name="xeb", align_bytes=64)
            xeb = cur["xeb"]
            wc, wp = blocks[("we", gg)]
            xc, xp = blocks[("x", tb)]
            acc = ps_a.tile([P, 512], F32, tag="acc", name="acc")
            mm4(acc, wc, wp, P * t, xc, xp)
            post = blocks[("pos", tb)]
            pos_t = post[:, gg, :].rearrange("p (r t) -> p r t", t=4)[:, :, t]
            nc.vector.scalar_tensor_tensor(
                out=xeb[:, t, :].rearrange("p (b r) -> p b r", b=2),
                in0=acc[:].rearrange("p (b r) -> p b r", b=2),
                scalar=be[:, 4 * gg + t : 4 * gg + t + 1],
                in1=pos_t.unsqueeze(1).to_broadcast([P, 2, 256]),
                op0=ADD,
                op1=ADD,
            )
            after_unit()
            if t == 3:
                pend_s.append(lambda: interleave(tb, gg, xeb))

        def emit_s2(wb, tt):
            tb = tt // 4
            q = tt % 4
            if tt == 0:
                need_block(("w", wb))
            if q == 0:
                flush_s()
                need_block(("xe", tb))
            if q % 2 == 0:
                cur["ost"] = p_st.tile([P, 2, 512], F32, tag="st", name="ost", align_bytes=64)
            ost = cur["ost"]
            xc, xp = blocks[("xe", tb)]
            wc, wp = blocks[("w", wb)]
            acc = ps_a.tile([P, 512], F32, tag="acc", name="acc")
            mm4(acc, xc, xp, P * q, wc, wp)
            nc.vector.tensor_tensor(
                out=ost[:, q % 2, :], in0=acc[:], in1=bias[:, 512 * wb : 512 * wb + 512], op=ADD
            )
            after_unit()
            if q % 2 == 1:
                r0 = (q // 2) * NPOS + tb * 256
                c0 = (wb % 4) * 512
                nc.sync.dma_start(
                    out=outs[wb // 4][r0 : r0 + 256, c0 : c0 + 512].rearrange(
                        "(h p) c -> p h c", p=P
                    ),
                    in_=ost[:],
                )

        srs = []
        i = 0
        while i < len(runs):
            if runs[i]["kind"] == "pos":
                srs.append([i])
                i = i + 1
            else:
                srs.append([i, i + 1])
                i = i + 2
        for i in range(4):
            emit_load(i)
        emit_sort(0)
        emit_sort(1)
        nxt = [0]

        def sr_next():
            emit_sr(nxt[0])
            nxt[0] = nxt[0] + 1

        for i in range(4):
            sr_next()
        nc.vector.tensor_copy(out=be[:], in_=be_raw[:].rearrange("p g t -> p (g t)"))
        for gg in range(4):
            for t in range(4):
                if gg == 3 and t == 2:
                    sr_next()
                emit_s1(0, gg, t)
            if gg < 3:
                sr_next()
        for tb in range(1, NTB):
            for gg in range(4):
                if gg == 0 or (gg == 2 and tb < NTB - 1):
                    sr_next()
                if tb == 2 and gg == 3:
                    for wi in range(3):
                        nc.sync.dma_start(
                            out=bias[:, wi * E : (wi + 1) * E], in_=b2[wi].partition_broadcast(P)
                        )
                for t in range(4):
                    emit_s1(tb, gg, t)
        for wb in range(12):
            for tt in range(32):
                if wb < 11 and tt == 0:
                    sr_next()
                emit_s2(wb, tt)
